import numpy as np
import ml_dtypes


def mxq(x, axis, fmt="e4m3"):
    dtype, down = {"e4m3": (ml_dtypes.float8_e4m3fn, 7), "e5m2": (ml_dtypes.float8_e5m2, 14)}[fmt]
    v = np.moveaxis(np.asarray(x, np.float32).astype(ml_dtypes.bfloat16).astype(np.float64), axis, -1)
    blocks = v.reshape(v.shape[:-1] + (-1, 32))
    amax = np.abs(blocks).max(-1, keepdims=True)
    byte = np.maximum(np.where(amax > 0, np.frexp(amax)[1] - 1 + 127, 0) - down, 1)
    scale = np.exp2(byte - 127.0)
    codes = (blocks / scale).astype(np.float32).astype(dtype).astype(np.float64)
    return np.moveaxis((codes * scale).reshape(v.shape), -1, axis)


WIDE = False


def mx_kscale(k):
    if not WIDE:
        return np.ones(k)
    levels = np.array([10, -10, 5, -5, 0])
    a = np.random.permutation(np.resize(levels, k // 512 * 4)).reshape(k // 512, 4)
    idx = np.arange(k)
    return np.exp2(a[idx // 512, idx % 128 // 32])


BF16 = ml_dtypes.bfloat16


def bf(x):
    return np.asarray(x, np.float32).astype(BF16)


def f64(x):
    return np.asarray(x).astype(np.float64)


E2M1 = np.array([0.0, 0.5, 1.0, 1.5, 2.0, 3.0, 4.0, 6.0, -0.0, -0.5, -1.0, -1.5, -2.0, -3.0, -4.0, -6.0])


def pack_weight(w, fmt):
    k, n = w.shape
    w = f64(bf(w)).reshape(k // 32, 32, n)
    amax = np.abs(w).max(1)
    if fmt == "e4m3":
        byte = np.frexp(amax)[1] - 1 + 127 - 7
    else:
        mant, ex = np.frexp(amax / 6.0)
        byte = np.where(mant > 0.5, ex, ex - 1) + 127
    byte = np.clip(np.where(amax > 0, byte, 1), 1, 254)
    scaled = (w * np.exp2(127.0 - byte)[:, None, :]).reshape(k, n).astype(np.float32)
    by_word = np.ascontiguousarray(scaled.reshape(k // 512, 128, 4, n).transpose(0, 1, 3, 2))
    if fmt == "e4m3":
        words = by_word.astype(ml_dtypes.float8_e4m3fn).view(np.uint8)
    else:
        c = by_word.astype(ml_dtypes.float4_e2m1fn).view(np.uint8) & 0xF
        words = c[..., 0::2] | (c[..., 1::2] << 4)
    return np.ascontiguousarray(words), np.ascontiguousarray(byte.astype(np.uint8).reshape(k // 512, 16, n))


def unpack_weight(words, scales, fmt):
    g, p, n, _ = words.shape
    if fmt == "e4m3":
        vals = np.ascontiguousarray(words).view(ml_dtypes.float8_e4m3fn).astype(np.float64)
    else:
        nib = np.empty((g, p, n, 4), np.uint8)
        nib[..., 0::2] = words & 0xF
        nib[..., 1::2] = words >> 4
        vals = E2M1[nib]
    vals = vals * np.repeat(np.exp2(scales.astype(np.float64) - 127.0), 8, axis=1)[..., None]
    return vals.transpose(0, 1, 3, 2).reshape(g * 512, n)

def pack4(w):
    words, scales = pack_weight(w, "e2m1")
    return words.reshape(words.shape[0], 128, -1), scales


def unpack4(words, scales):
    return unpack_weight(words.reshape(words.shape[0], 128, -1, 2), scales, "e2m1")


N, N_CH, X, H = 512, 5, 512, 512
K = N_CH * H


def sigmoid(v):
    return 1.0 / (1.0 + np.exp(-v))


def setup_inputs():
    s, t = mx_kscale(X), mx_kscale(K)
    x = bf(np.random.standard_normal((N, X)) * s)
    x_mask = bf(np.random.random(N) < 0.75)
    neighbour_h = bf(np.random.standard_normal((N, N_CH, H)) * t.reshape(N_CH, H))
    neighbour_c = bf(np.random.standard_normal((N, N_CH, H)))
    W_f_in_words, W_f_in_scales = pack4(np.random.standard_normal((X, H)) * 0.5 / np.sqrt(X) / s[:, None])
    b_f_in = bf(np.random.standard_normal(H) * 0.3)
    W_aggr_f_words, W_aggr_f_scales = pack4(np.random.standard_normal((K, K)) / np.sqrt(K) / t[:, None])
    b_aggr_f = bf(np.random.standard_normal(K) * 0.3)
    return {
        "x": x,
        "x_mask": x_mask,
        "neighbour_h": neighbour_h,
        "neighbour_c": neighbour_c,
        "W_f_in_words": W_f_in_words,
        "W_f_in_scales": W_f_in_scales,
        "b_f_in": b_f_in,
        "W_aggr_f_words": W_aggr_f_words,
        "W_aggr_f_scales": W_aggr_f_scales,
        "b_aggr_f": b_aggr_f,
    }


def reference(x, x_mask, neighbour_h, neighbour_c, W_f_in_words, W_f_in_scales, b_f_in, W_aggr_f_words, W_aggr_f_scales, b_aggr_f):
    h_flat = f64(neighbour_h).reshape(N, K)
    f_input = ((mxq(f64(x), 1, "e4m3") @ unpack4(W_f_in_words, W_f_in_scales)) + f64(b_f_in)) * f64(x_mask)[:, None]
    f_input = np.tile(f_input, (1, N_CH))
    f_gate = (mxq(h_flat, 1, "e4m3") @ unpack4(W_aggr_f_words, W_aggr_f_scales)) + f64(b_aggr_f) + f_input
    f_aggr = f_gate + f_input
    f = sigmoid(f_aggr).reshape(N, N_CH, H)
    return np.sum(f * f64(neighbour_c), axis=1)

@@ -1,0 +1,222 @@
+from contextlib import ExitStack
+
+import concourse.mybir as mybir
+from concourse.masks import make_identity
+
+F32 = mybir.dt.float32
+BF16 = mybir.dt.bfloat16
+I32 = mybir.dt.int32
+U32 = mybir.dt.uint32
+U8 = mybir.dt.uint8
+FP8X4 = mybir.dt.float8_e4m3fn_x4
+FP4X4 = mybir.dt.float4_e2m1fn_x4
+ADD = mybir.AluOpType.add
+MULT = mybir.AluOpType.mult
+SIGMOID = mybir.ActivationFunctionType.Sigmoid
+
+P = 128
+NODES = 512
+CHILDREN = 5
+FEAT = 512
+K_PASS = 512
+NODE_TILES = NODES // P
+FEAT_TILES = FEAT // P
+COL_TILES = CHILDREN * FEAT_TILES
+FP4_BYTES = 2
+
+FLOPS = 2 * NODES * (CHILDREN * FEAT) * (CHILDREN * FEAT) + 2 * NODES * FEAT * FEAT
+
+
+def tile_treelstmcell_pa_kernel(
+    tc,
+    x,
+    x_mask,
+    neighbour_h,
+    neighbour_c,
+    W_f_in_words,
+    W_f_in_scales,
+    b_f_in,
+    W_aggr_f_words,
+    W_aggr_f_scales,
+    b_aggr_f,
+    out,
+):
+    nc = tc.nc
+    with ExitStack() as ctx:
+        ctx.enter_context(tc.manual_schedule())
+        keep = ctx.enter_context(tc.tile_pool(name="keep", bufs=1))
+        work = ctx.enter_context(tc.tile_pool(name="work", bufs=3))
+        psum_acc = ctx.enter_context(tc.psum_pool(name="psum_acc", bufs=4))
+        psum_aux = ctx.enter_context(tc.psum_pool(name="psum_aux", bufs=4))
+
+        ident_f32 = keep.tile([P, P], F32)
+        ident_bf16 = keep.tile([P, P], BF16)
+        ones_bf16 = keep.tile([P, P], BF16)
+        bias_rows = keep.tile([P, P], BF16)
+        bias_cols = keep.tile([P, P], F32)
+        mask_row = keep.tile([P, NODES], BF16)
+        mask_all = keep.tile([P, NODES], F32)
+        warm = keep.tile([P, 1], F32)
+
+        x_sb = keep.tile([P, NODE_TILES, FEAT], BF16)
+        h_sb = [keep.tile([P, NODE_TILES, FEAT], BF16, name="h_sb%d" % g) for g in range(CHILDREN)]
+        c_sb = [keep.tile([P, NODE_TILES, FEAT], BF16, name="c_sb%d" % k) for k in range(CHILDREN)]
+        wf_words = keep.tile([P, FP4_BYTES * FEAT], U8, align_bytes=64)
+        wf_scales = keep.tile([P, FEAT], U8, align_bytes=64)
+        wa_words = [
+            keep.tile([P, CHILDREN, FP4_BYTES * FEAT], U8, name="wa_words%d" % k, align_bytes=64)
+            for k in range(CHILDREN)
+        ]
+        wa_scales = keep.tile([P, CHILDREN, CHILDREN * FEAT], U8, align_bytes=64)
+
+        x_codes = keep.tile([P, NODES], U32, align_bytes=64)
+        x_scales = keep.tile([P, NODES], U8, align_bytes=64)
+        h_codes = keep.tile([P, CHILDREN, NODES], U32, align_bytes=64)
+        h_scales = keep.tile([P, CHILDREN, NODES], U8, align_bytes=64)
+
+        f_input = keep.tile([P, FEAT_TILES, NODES], F32)
+        total = keep.tile([P, FEAT_TILES, NODES], F32)
+
+        nc.vector.memset(warm[:], 0.0)
+        nc.vector.memset(bias_rows[:], 0.0)
+        nc.vector.memset(mask_row[:], 0.0)
+        nc.vector.memset(ones_bf16[:], 1.0)
+        nc.vector.memset(wf_scales[:].bitcast(I32), 0)
+        nc.vector.memset(wa_scales[:].rearrange("p g n -> p (g n)").bitcast(I32), 0)
+        make_identity(nc, ident_f32[:])
+        make_identity(nc, ident_bf16[:])
+        nc.scalar.activation(out=warm[:], in_=warm[:], func=SIGMOID)
+
+        nc.sync.dma_start(out=x_sb[:], in_=x.rearrange("(i p) k -> p i k", p=P))
+        nc.sync.dma_start(out=bias_rows[0:COL_TILES, :], in_=b_aggr_f.rearrange("(r c) -> r c", c=P))
+        nc.sync.dma_start(
+            out=bias_rows[COL_TILES : COL_TILES + FEAT_TILES, :], in_=b_f_in.rearrange("(r c) -> r c", c=P)
+        )
+        nc.sync.dma_start(out=mask_row[0:1, :], in_=x_mask.rearrange("(o n) -> o n", o=1))
+        nc.sync.dma_start(out=wf_words[:].bitcast(I32), in_=W_f_in_words[0].bitcast(I32))
+        for g in range(CHILDREN):
+            nc.sync.dma_start(out=h_sb[g][:], in_=neighbour_h[:, g, :].rearrange("(i p) k -> p i k", p=P))
+        wa_words_dram = W_aggr_f_words.rearrange("g p b -> p g b")
+        for k in range(CHILDREN):
+            cols = slice(k * FP4_BYTES * FEAT, (k + 1) * FP4_BYTES * FEAT)
+            nc.sync.dma_start(out=wa_words[k][:].bitcast(I32), in_=wa_words_dram[:, :, cols].bitcast(I32))
+            nc.sync.dma_start(out=c_sb[k][:], in_=neighbour_c[:, k, :].rearrange("(i p) j -> p i j", p=P))
+        for r in range(4):
+            nc.gpsimd.dma_start(
+                out=wf_scales[r:P:32, :].bitcast(F32), in_=W_f_in_scales[0, r:16:4, :].bitcast(F32)
+            )
+        wa_scales_dram = W_aggr_f_scales.rearrange("g q n -> q g n")
+        for r in range(4):
+            nc.gpsimd.dma_start(
+                out=wa_scales[r:P:32, :, :].bitcast(F32), in_=wa_scales_dram[r:16:4, :, :].bitcast(F32)
+            )
+
+        bias_ps = psum_aux.tile([P, P], BF16, tag="aux")
+        nc.tensor.transpose(bias_ps[:], bias_rows[:], ident_bf16[:])
+        nc.vector.tensor_copy(out=bias_cols[:], in_=bias_ps[:])
+        mask_ps = psum_aux.tile([P, NODES], F32, tag="aux")
+        nc.tensor.matmul(mask_ps[:], lhsT=ones_bf16[:], rhs=mask_row[:], start=True, stop=True)
+        nc.scalar.copy(out=mask_all[:], in_=mask_ps[:])
+
+        def quantise_512_k(rows_sb, codes, scales):
+            grouped = work.tile([P, NODES * 4], BF16, tag="grouped", align_bytes=64)
+            grouped_words = grouped[:].bitcast(F32).rearrange("p (n u) -> p n u", u=2)
+            for half in range(2):
+                flipped = psum_aux.tile([P, 2, 2 * P], F32, tag="aux")
+                for i2 in range(2):
+                    words = rows_sb[:, 2 * half + i2, :].bitcast(F32)
+                    for u in range(2):
+                        nc.tensor.transpose(
+                            flipped[:, u, i2 * P : (i2 + 1) * P], words[:, u : FEAT // 2 : 2], ident_f32[:]
+                        )
+                dst = grouped_words[:, half * 2 * P : (half + 1) * 2 * P, :]
+                src = flipped[:].rearrange("p u n -> p n u")
+                if half == 0:
+                    nc.scalar.copy(out=dst, in_=src)
+                else:
+                    nc.vector.tensor_copy(out=dst, in_=src)
+            nc.vector.quantize_mx(out=codes.bitcast(FP8X4), scales=scales, in_=grouped[:])
+
+        quantise_512_k(x_sb, x_codes[:], x_scales[:])
+        for g in range(CHILDREN):
+            quantise_512_k(h_sb[g], h_codes[:, g, :], h_scales[:, g, :])
+
+        for jt in range(FEAT_TILES):
+            acc = psum_acc.tile([P, NODES], F32, tag="acc")
+            nc.tensor.matmul_mx(
+                out=acc[:],
+                lhsT=wf_words[:, jt * FP4_BYTES * P : (jt + 1) * FP4_BYTES * P].bitcast(FP4X4),
+                lhsT_scale=wf_scales[:, jt * P : (jt + 1) * P],
+                rhs=x_codes[:].bitcast(FP8X4),
+                rhs_scale=x_scales[:],
+                start=True,
+                stop=True,
+            )
+            nc.vector.scalar_tensor_tensor(
+                out=f_input[:, jt, :],
+                in0=acc[:],
+                scalar=bias_cols[:, COL_TILES + jt : COL_TILES + jt + 1],
+                in1=mask_all[:],
+                op0=ADD,
+                op1=MULT,
+            )
+
+        gates = {}
+        c_flipped = {}
+
+        def gate(ct):
+            k, jt = divmod(ct, FEAT_TILES)
+            acc = psum_acc.tile([P, NODES], F32, tag="acc")
+            for g in range(CHILDREN):
+                nc.tensor.matmul_mx(
+                    out=acc[:],
+                    lhsT=wa_words[k][:, g, jt * FP4_BYTES * P : (jt + 1) * FP4_BYTES * P].bitcast(FP4X4),
+                    lhsT_scale=wa_scales[:, g, ct * P : (ct + 1) * P],
+                    rhs=h_codes[:, g, :].bitcast(FP8X4),
+                    rhs_scale=h_scales[:, g, :],
+                    start=(g == 0),
+                    stop=(g == CHILDREN - 1),
+                )
+            if ct % 2 == 0:
+                pair = psum_aux.tile([P, 2, NODES], BF16, tag="aux")
+                for j2 in range(2):
+                    for i in range(NODE_TILES):
+                        nc.tensor.matmul(
+                            pair[:, j2, i * P : (i + 1) * P],
+                            lhsT=c_sb[k][:, i, (jt + j2) * P : (jt + j2 + 1) * P],
+                            rhs=ident_bf16[:],
+                            start=True,
+                            stop=True,
+                        )
+                    c_flipped[ct + j2] = pair[:, j2, :]
+            z = work.tile([P, NODES], F32, tag="z")
+            nc.vector.scalar_tensor_tensor(
+                out=z[:], in0=f_input[:, jt, :], scalar=2.0, in1=acc[:], op0=MULT, op1=ADD
+            )
+            f = work.tile([P, NODES], F32, tag="f")
+            nc.scalar.activation(out=f[:], in_=z[:], func=SIGMOID, bias=bias_cols[:, ct : ct + 1], scale=1.0)
+            gates[ct] = f
+
+        def weigh_and_add(ct):
+            k, jt = divmod(ct, FEAT_TILES)
+            if k == 0:
+                nc.vector.tensor_tensor(out=total[:, jt, :], in0=gates[ct][:], in1=c_flipped[ct], op=MULT)
+            else:
+                term = work.tile([P, NODES], F32, tag="term")
+                nc.vector.tensor_tensor(out=term[:], in0=gates[ct][:], in1=c_flipped[ct], op=MULT)
+                nc.gpsimd.tensor_tensor(out=total[:, jt, :], in0=total[:, jt, :], in1=term[:], op=ADD)
+
+        gate(0)
+        for ct in range(1, COL_TILES):
+            gate(ct)
+            weigh_and_add(ct - 1)
+        weigh_and_add(COL_TILES - 1)
+
+        out_view = out.rearrange("(i p) j -> p i j", p=P)
+        for jt in range(FEAT_TILES):
+            back = psum_aux.tile([P, NODE_TILES, P], F32, tag="aux")
+            for i in range(NODE_TILES):
+                nc.tensor.transpose(back[:, i, :], total[:, jt, i * P : (i + 1) * P], ident_f32[:])
+            result = work.tile([P, NODE_TILES, P], F32, tag="result")
+            nc.scalar.copy(out=result[:], in_=back[:])
+            nc.sync.dma_start(out=out_view[:, :, jt * P : (jt + 1) * P], in_=result[:])

@@ -80,43 +80,46 @@ def tile_treelstmcell_pa_kernel(
         nc.vector.memset(warm[:], 0.0)
         nc.vector.memset(bias_rows[:], 0.0)
         nc.vector.memset(mask_row[:], 0.0)
-        nc.vector.memset(ones_bf16[:], 1.0)
         nc.vector.memset(wf_scales[:].bitcast(I32), 0)
         nc.vector.memset(wa_scales[:].rearrange("p g n -> p (g n)").bitcast(I32), 0)
+        nc.vector.memset(ones_bf16[:], 1.0)
         make_identity(nc, ident_f32[:])
         make_identity(nc, ident_bf16[:])
         nc.scalar.activation(out=warm[:], in_=warm[:], func=SIGMOID)
 
-        nc.sync.dma_start(out=x_sb[:], in_=x.rearrange("(i p) k -> p i k", p=P))
-        nc.sync.dma_start(out=bias_rows[0:COL_TILES, :], in_=b_aggr_f.rearrange("(r c) -> r c", c=P))
-        nc.sync.dma_start(
+        nc.gpsimd.dma_start(out=bias_rows[0:COL_TILES, :], in_=b_aggr_f.rearrange("(r c) -> r c", c=P))
+        nc.gpsimd.dma_start(
             out=bias_rows[COL_TILES : COL_TILES + FEAT_TILES, :], in_=b_f_in.rearrange("(r c) -> r c", c=P)
         )
-        nc.sync.dma_start(out=mask_row[0:1, :], in_=x_mask.rearrange("(o n) -> o n", o=1))
-        nc.sync.dma_start(out=wf_words[:].bitcast(I32), in_=W_f_in_words[0].bitcast(I32))
-        for g in range(CHILDREN):
-            nc.sync.dma_start(out=h_sb[g][:], in_=neighbour_h[:, g, :].rearrange("(i p) k -> p i k", p=P))
+        nc.gpsimd.dma_start(out=mask_row[0:1, :], in_=x_mask.rearrange("(o n) -> o n", o=1))
+
         wa_words_dram = W_aggr_f_words.rearrange("g p b -> p g b")
-        for k in range(CHILDREN):
+        wa_scales_dram = W_aggr_f_scales.rearrange("g q n -> q g n")
+
+        def load_child_words(k):
             cols = slice(k * FP4_BYTES * FEAT, (k + 1) * FP4_BYTES * FEAT)
             nc.sync.dma_start(out=wa_words[k][:].bitcast(I32), in_=wa_words_dram[:, :, cols].bitcast(I32))
-            nc.sync.dma_start(out=c_sb[k][:], in_=neighbour_c[:, k, :].rearrange("(i p) j -> p i j", p=P))
-        for r in range(4):
-            nc.gpsimd.dma_start(
-                out=wf_scales[r:P:32, :].bitcast(F32), in_=W_f_in_scales[0, r:16:4, :].bitcast(F32)
-            )
-        wa_scales_dram = W_aggr_f_scales.rearrange("g q n -> q g n")
-        for r in range(4):
-            nc.gpsimd.dma_start(
-                out=wa_scales[r:P:32, :, :].bitcast(F32), in_=wa_scales_dram[r:16:4, :, :].bitcast(F32)
-            )
 
-        bias_ps = psum_aux.tile([P, P], BF16, tag="aux")
-        nc.tensor.transpose(bias_ps[:], bias_rows[:], ident_bf16[:])
-        nc.vector.tensor_copy(out=bias_cols[:], in_=bias_ps[:])
-        mask_ps = psum_aux.tile([P, NODES], F32, tag="aux")
-        nc.tensor.matmul(mask_ps[:], lhsT=ones_bf16[:], rhs=mask_row[:], start=True, stop=True)
-        nc.scalar.copy(out=mask_all[:], in_=mask_ps[:])
+        def load_child_c(k):
+            nc.sync.dma_start(out=c_sb[k][:], in_=neighbour_c[:, k, :].rearrange("(i p) j -> p i j", p=P))
+
+        nc.sync.dma_start(out=x_sb[:], in_=x.rearrange("(i p) k -> p i k", p=P))
+        for g in range(CHILDREN):
+            nc.sync.dma_start(out=h_sb[g][:], in_=neighbour_h[:, g, :].rearrange("(i p) k -> p i k", p=P))
+        load_child_words(0)
+        nc.sync.dma_start(out=wf_words[:].bitcast(I32), in_=W_f_in_words[0].bitcast(I32))
+        for r in range(4):
+            nc.sync.dma_start(
+                out=wf_scales[r:P:32, :].bitcast(I32), in_=W_f_in_scales[0, r:16:4, :].bitcast(I32)
+            )
+        for r in range(4):
+            nc.sync.dma_start(
+                out=wa_scales[r:P:32, :, :].bitcast(I32), in_=wa_scales_dram[r:16:4, :, :].bitcast(I32)
+            )
+        load_child_c(0)
+        for k in range(1, CHILDREN):
+            load_child_words(k)
+            load_child_c(k)
 
         def quantise_512_k(rows_sb, codes, scales):
             grouped = work.tile([P, NODES * 4], BF16, tag="grouped", align_bytes=64)
@@ -141,8 +144,15 @@ def tile_treelstmcell_pa_kernel(
         for g in range(CHILDREN):
             quantise_512_k(h_sb[g], h_codes[:, g, :], h_scales[:, g, :])
 
+        bias_ps = psum_aux.tile([P, P], BF16, tag="aux")
+        nc.tensor.transpose(bias_ps[:], bias_rows[:], ident_bf16[:])
+        nc.vector.tensor_copy(out=bias_cols[:], in_=bias_ps[:])
+        mask_ps = psum_aux.tile([P, NODES], F32, tag="aux")
+        nc.tensor.matmul(mask_ps[:], lhsT=ones_bf16[:], rhs=mask_row[:], start=True, stop=True)
+        nc.scalar.copy(out=mask_all[:], in_=mask_ps[:])
+
         for jt in range(FEAT_TILES):
-            acc = psum_acc.tile([P, NODES], F32, tag="acc")
+            acc = psum_aux.tile([P, NODES], F32, tag="aux")
             nc.tensor.matmul_mx(
                 out=acc[:],
                 lhsT=wf_words[:, jt * FP4_BYTES * P : (jt + 1) * FP4_BYTES * P].bitcast(FP4X4),
@@ -204,7 +214,8 @@ def tile_treelstmcell_pa_kernel(
             else:
                 term = work.tile([P, NODES], F32, tag="term")
                 nc.vector.tensor_tensor(out=term[:], in0=gates[ct][:], in1=c_flipped[ct], op=MULT)
-                nc.gpsimd.tensor_tensor(out=total[:, jt, :], in0=total[:, jt, :], in1=term[:], op=ADD)
+                adder = nc.vector if ct == COL_TILES - 1 else nc.gpsimd
+                adder.tensor_tensor(out=total[:, jt, :], in0=total[:, jt, :], in1=term[:], op=ADD)
 
         gate(0)
         for ct in range(1, COL_TILES):
@@ -218,5 +229,8 @@ def tile_treelstmcell_pa_kernel(
             for i in range(NODE_TILES):
                 nc.tensor.transpose(back[:, i, :], total[:, jt, i * P : (i + 1) * P], ident_f32[:])
             result = work.tile([P, NODE_TILES, P], F32, tag="result")
-            nc.scalar.copy(out=result[:], in_=back[:])
+            if jt % 2 == 0:
+                nc.scalar.copy(out=result[:], in_=back[:])
+            else:
+                nc.vector.tensor_copy(out=result[:], in_=back[:])
             nc.sync.dma_start(out=out_view[:, :, jt * P : (jt + 1) * P], in_=result[:])

@@ -45,6 +45,7 @@ def tile_treelstmcell_pa_kernel(
     with ExitStack() as ctx:
         ctx.enter_context(tc.manual_schedule())
         keep = ctx.enter_context(tc.tile_pool(name="keep", bufs=1))
+        stage = ctx.enter_context(tc.tile_pool(name="stage", bufs=4))
         work = ctx.enter_context(tc.tile_pool(name="work", bufs=3))
         psum_acc = ctx.enter_context(tc.psum_pool(name="psum_acc", bufs=4))
         psum_aux = ctx.enter_context(tc.psum_pool(name="psum_aux", bufs=4))
@@ -59,7 +60,7 @@ def tile_treelstmcell_pa_kernel(
         warm = keep.tile([P, 1], F32)
 
         x_sb = keep.tile([P, NODE_TILES, FEAT], BF16)
-        h_sb = [keep.tile([P, NODE_TILES, FEAT], BF16, name="h_sb%d" % g) for g in range(CHILDREN)]
+        h_sb = [keep.tile([P, CHILDREN, FEAT], BF16, name="h_sb%d" % i) for i in range(NODE_TILES)]
         c_sb = [keep.tile([P, NODE_TILES, FEAT], BF16, name="c_sb%d" % k) for k in range(CHILDREN)]
         wf_words = keep.tile([P, FP4_BYTES * FEAT], U8, align_bytes=64)
         wf_scales = keep.tile([P, FEAT], U8, align_bytes=64)
@@ -93,63 +94,68 @@ def tile_treelstmcell_pa_kernel(
         )
         nc.gpsimd.dma_start(out=mask_row[0:1, :], in_=x_mask.rearrange("(o n) -> o n", o=1))
 
+        h_dram = neighbour_h.rearrange("(p i) g k -> p i g k", i=NODE_TILES)
+        c_dram = neighbour_c.rearrange("(p i) k j -> p i k j", i=NODE_TILES)
         wa_words_dram = W_aggr_f_words.rearrange("g p b -> p g b")
         wa_scales_dram = W_aggr_f_scales.rearrange("g q n -> q g n")
 
-        def load_child_words(k):
-            cols = slice(k * FP4_BYTES * FEAT, (k + 1) * FP4_BYTES * FEAT)
-            nc.sync.dma_start(out=wa_words[k][:].bitcast(I32), in_=wa_words_dram[:, :, cols].bitcast(I32))
-
-        def load_child_c(k):
-            nc.sync.dma_start(out=c_sb[k][:], in_=neighbour_c[:, k, :].rearrange("(i p) j -> p i j", p=P))
-
-        nc.sync.dma_start(out=x_sb[:], in_=x.rearrange("(i p) k -> p i k", p=P))
-        for g in range(CHILDREN):
-            nc.sync.dma_start(out=h_sb[g][:], in_=neighbour_h[:, g, :].rearrange("(i p) k -> p i k", p=P))
-        load_child_words(0)
+        nc.sync.dma_start(out=x_sb[:], in_=x.rearrange("(p i) k -> p i k", i=NODE_TILES))
+        for i in range(NODE_TILES):
+            nc.sync.dma_start(out=h_sb[i][:], in_=h_dram[:, i, :, :])
         nc.sync.dma_start(out=wf_words[:].bitcast(I32), in_=W_f_in_words[0].bitcast(I32))
         for r in range(4):
             nc.sync.dma_start(
                 out=wf_scales[r:P:32, :].bitcast(I32), in_=W_f_in_scales[0, r:16:4, :].bitcast(I32)
             )
-        for r in range(4):
-            nc.sync.dma_start(
-                out=wa_scales[r:P:32, :, :].bitcast(I32), in_=wa_scales_dram[r:16:4, :, :].bitcast(I32)
-            )
-        load_child_c(0)
-        for k in range(1, CHILDREN):
-            load_child_words(k)
-            load_child_c(k)
+        for k in range(CHILDREN):
+            cols = slice(k * FP4_BYTES * FEAT, (k + 1) * FP4_BYTES * FEAT)
+            nc.sync.dma_start(out=wa_words[k][:].bitcast(I32), in_=wa_words_dram[:, :, cols].bitcast(I32))
+            for r in range(4):
+                nc.sync.dma_start(
+                    out=wa_scales[r:P:32, :, k * FEAT : (k + 1) * FEAT].bitcast(I32),
+                    in_=wa_scales_dram[r:16:4, :, k * FEAT : (k + 1) * FEAT].bitcast(I32),
+                )
+            nc.sync.dma_start(out=c_sb[k][:], in_=c_dram[:, :, k, :])
 
-        def quantise_512_k(rows_sb, codes, scales):
-            grouped = work.tile([P, NODES * 4], BF16, tag="grouped", align_bytes=64)
-            grouped_words = grouped[:].bitcast(F32).rearrange("p (n u) -> p n u", u=2)
-            for half in range(2):
-                flipped = psum_aux.tile([P, 2, 2 * P], F32, tag="aux")
-                for i2 in range(2):
-                    words = rows_sb[:, 2 * half + i2, :].bitcast(F32)
-                    for u in range(2):
-                        nc.tensor.transpose(
-                            flipped[:, u, i2 * P : (i2 + 1) * P], words[:, u : FEAT // 2 : 2], ident_f32[:]
-                        )
-                dst = grouped_words[:, half * 2 * P : (half + 1) * 2 * P, :]
-                src = flipped[:].rearrange("p u n -> p n u")
-                if half == 0:
-                    nc.scalar.copy(out=dst, in_=src)
-                else:
-                    nc.vector.tensor_copy(out=dst, in_=src)
-            nc.vector.quantize_mx(out=codes.bitcast(FP8X4), scales=scales, in_=grouped[:])
+        units = []
+        for i in range(NODE_TILES):
+            nodes = slice(i * P, (i + 1) * P)
+            units.append((x_sb[:, i, :], x_codes[:, nodes], x_scales[:, nodes]))
+        for i in range(NODE_TILES):
+            nodes = slice(i * P, (i + 1) * P)
+            for g in range(CHILDREN):
+                units.append((h_sb[i][:, g, :], h_codes[:, g, nodes], h_scales[:, g, nodes]))
 
-        quantise_512_k(x_sb, x_codes[:], x_scales[:])
-        for g in range(CHILDREN):
-            quantise_512_k(h_sb[g], h_codes[:, g, :], h_scales[:, g, :])
+        def quantise_two_units(two_units, copy_engine_is_vector):
+            flipped = psum_aux.tile([P, 2, 2, P], F32, tag="aux")
+            grouped = stage.tile([P, 2, K_PASS], BF16, tag="grouped", align_bytes=64)
+            for a in range(2):
+                words = two_units[a][0].bitcast(F32)
+                for u in range(2):
+                    nc.tensor.transpose(flipped[:, a, u, :], words[:, u : K_PASS // 2 : 2], ident_f32[:])
+            dst = grouped[:].bitcast(F32).rearrange("p a (n u) -> p a n u", u=2)
+            src = flipped[:].rearrange("p a u n -> p a n u")
+            if copy_engine_is_vector:
+                nc.vector.tensor_copy(out=dst, in_=src)
+            else:
+                nc.scalar.copy(out=dst, in_=src)
+            for a in range(2):
+                nc.vector.quantize_mx(
+                    out=two_units[a][1].bitcast(FP8X4), scales=two_units[a][2], in_=grouped[:, a, :]
+                )
+
+        for bank in range(len(units) // 2):
+            quantise_two_units(units[2 * bank : 2 * bank + 2], bank % 3 == 2)
 
         bias_ps = psum_aux.tile([P, P], BF16, tag="aux")
         nc.tensor.transpose(bias_ps[:], bias_rows[:], ident_bf16[:])
         nc.vector.tensor_copy(out=bias_cols[:], in_=bias_ps[:])
         mask_ps = psum_aux.tile([P, NODES], F32, tag="aux")
         nc.tensor.matmul(mask_ps[:], lhsT=ones_bf16[:], rhs=mask_row[:], start=True, stop=True)
-        nc.scalar.copy(out=mask_all[:], in_=mask_ps[:])
+        nc.scalar.copy(
+            out=mask_all[:].rearrange("q (i p) -> q i p", i=NODE_TILES),
+            in_=mask_ps[:].rearrange("q (p i) -> q i p", i=NODE_TILES),
+        )
 
         for jt in range(FEAT_TILES):
             acc = psum_aux.tile([P, NODES], F32, tag="aux")
@@ -223,7 +229,7 @@ def tile_treelstmcell_pa_kernel(
             weigh_and_add(ct - 1)
         weigh_and_add(COL_TILES - 1)
 
-        out_view = out.rearrange("(i p) j -> p i j", p=P)
+        out_view = out.rearrange("(p i) j -> p i j", i=NODE_TILES)
         for jt in range(FEAT_TILES):
             back = psum_aux.tile([P, NODE_TILES, P], F32, tag="aux")
             for i in range(NODE_TILES):

@@ -102,11 +102,6 @@ def tile_treelstmcell_pa_kernel(
         nc.sync.dma_start(out=x_sb[:], in_=x.rearrange("(p i) k -> p i k", i=NODE_TILES))
         for i in range(NODE_TILES):
             nc.sync.dma_start(out=h_sb[i][:], in_=h_dram[:, i, :, :])
-        nc.sync.dma_start(out=wf_words[:].bitcast(I32), in_=W_f_in_words[0].bitcast(I32))
-        for r in range(4):
-            nc.sync.dma_start(
-                out=wf_scales[r:P:32, :].bitcast(I32), in_=W_f_in_scales[0, r:16:4, :].bitcast(I32)
-            )
         for k in range(CHILDREN):
             cols = slice(k * FP4_BYTES * FEAT, (k + 1) * FP4_BYTES * FEAT)
             nc.sync.dma_start(out=wa_words[k][:].bitcast(I32), in_=wa_words_dram[:, :, cols].bitcast(I32))
@@ -115,6 +110,12 @@ def tile_treelstmcell_pa_kernel(
                     out=wa_scales[r:P:32, :, k * FEAT : (k + 1) * FEAT].bitcast(I32),
                     in_=wa_scales_dram[r:16:4, :, k * FEAT : (k + 1) * FEAT].bitcast(I32),
                 )
+            if k == 0:
+                nc.sync.dma_start(out=wf_words[:].bitcast(I32), in_=W_f_in_words[0].bitcast(I32))
+                for r in range(4):
+                    nc.sync.dma_start(
+                        out=wf_scales[r:P:32, :].bitcast(I32), in_=W_f_in_scales[0, r:16:4, :].bitcast(I32)
+                    )
             nc.sync.dma_start(out=c_sb[k][:], in_=c_dram[:, :, k, :])
 
         units = []
@@ -126,26 +127,37 @@ def tile_treelstmcell_pa_kernel(
             for g in range(CHILDREN):
                 units.append((h_sb[i][:, g, :], h_codes[:, g, nodes], h_scales[:, g, nodes]))
 
-        def quantise_two_units(two_units, copy_engine_is_vector):
+        banks = [units[first : first + 2] for first in range(0, len(units), 2)]
+        grouped_of_bank = {}
+
+        def flip_two_units(bank):
             flipped = psum_aux.tile([P, 2, 2, P], F32, tag="aux")
             grouped = stage.tile([P, 2, K_PASS], BF16, tag="grouped", align_bytes=64)
             for a in range(2):
-                words = two_units[a][0].bitcast(F32)
+                words = banks[bank][a][0].bitcast(F32)
                 for u in range(2):
                     nc.tensor.transpose(flipped[:, a, u, :], words[:, u : K_PASS // 2 : 2], ident_f32[:])
             dst = grouped[:].bitcast(F32).rearrange("p a (n u) -> p a n u", u=2)
             src = flipped[:].rearrange("p a u n -> p a n u")
-            if copy_engine_is_vector:
+            if bank % 3 == 2:
                 nc.vector.tensor_copy(out=dst, in_=src)
             else:
                 nc.scalar.copy(out=dst, in_=src)
+            grouped_of_bank[bank] = grouped
+
+        def quantise_two_units(bank):
             for a in range(2):
                 nc.vector.quantize_mx(
-                    out=two_units[a][1].bitcast(FP8X4), scales=two_units[a][2], in_=grouped[:, a, :]
+                    out=banks[bank][a][1].bitcast(FP8X4),
+                    scales=banks[bank][a][2],
+                    in_=grouped_of_bank[bank][:, a, :],
                 )
 
-        for bank in range(len(units) // 2):
-            quantise_two_units(units[2 * bank : 2 * bank + 2], bank % 3 == 2)
+        for bank in range(len(banks)):
+            flip_two_units(bank)
+            if bank > 0:
+                quantise_two_units(bank - 1)
+        quantise_two_units(len(banks) - 1)
 
         bias_ps = psum_aux.tile([P, P], BF16, tag="aux")
         nc.tensor.transpose(bias_ps[:], bias_rows[:], ident_bf16[:])
@@ -157,30 +169,32 @@ def tile_treelstmcell_pa_kernel(
             in_=mask_ps[:].rearrange("q (p i) -> q i p", i=NODE_TILES),
         )
 
-        for jt in range(FEAT_TILES):
-            acc = psum_aux.tile([P, NODES], F32, tag="aux")
-            nc.tensor.matmul_mx(
-                out=acc[:],
-                lhsT=wf_words[:, jt * FP4_BYTES * P : (jt + 1) * FP4_BYTES * P].bitcast(FP4X4),
-                lhsT_scale=wf_scales[:, jt * P : (jt + 1) * P],
-                rhs=x_codes[:].bitcast(FP8X4),
-                rhs_scale=x_scales[:],
-                start=True,
-                stop=True,
-            )
-            nc.vector.scalar_tensor_tensor(
-                out=f_input[:, jt, :],
-                in0=acc[:],
-                scalar=bias_cols[:, COL_TILES + jt : COL_TILES + jt + 1],
-                in1=mask_all[:],
-                op0=ADD,
-                op1=MULT,
-            )
+        def compute_f_input():
+            for jt in range(FEAT_TILES):
+                acc = psum_aux.tile([P, NODES], F32, tag="aux")
+                nc.tensor.matmul_mx(
+                    out=acc[:],
+                    lhsT=wf_words[:, jt * FP4_BYTES * P : (jt + 1) * FP4_BYTES * P].bitcast(FP4X4),
+                    lhsT_scale=wf_scales[:, jt * P : (jt + 1) * P],
+                    rhs=x_codes[:].bitcast(FP8X4),
+                    rhs_scale=x_scales[:],
+                    start=True,
+                    stop=True,
+                )
+                nc.vector.scalar_tensor_tensor(
+                    out=f_input[:, jt, :],
+                    in0=acc[:],
+                    scalar=bias_cols[:, COL_TILES + jt : COL_TILES + jt + 1],
+                    in1=mask_all[:],
+                    op0=ADD,
+                    op1=MULT,
+                )
 
+        sums = {}
         gates = {}
         c_flipped = {}
 
-        def gate(ct):
+        def gate_matmuls(ct):
             k, jt = divmod(ct, FEAT_TILES)
             acc = psum_acc.tile([P, NODES], F32, tag="acc")
             for g in range(CHILDREN):
@@ -193,21 +207,27 @@ def tile_treelstmcell_pa_kernel(
                     start=(g == 0),
                     stop=(g == CHILDREN - 1),
                 )
-            if ct % 2 == 0:
-                pair = psum_aux.tile([P, 2, NODES], BF16, tag="aux")
-                for j2 in range(2):
-                    for i in range(NODE_TILES):
-                        nc.tensor.matmul(
-                            pair[:, j2, i * P : (i + 1) * P],
-                            lhsT=c_sb[k][:, i, (jt + j2) * P : (jt + j2 + 1) * P],
-                            rhs=ident_bf16[:],
-                            start=True,
-                            stop=True,
-                        )
-                    c_flipped[ct + j2] = pair[:, j2, :]
+            sums[ct] = acc
+
+        def flip_c_of_two_tiles(ct):
+            k, jt = divmod(ct, FEAT_TILES)
+            pair = psum_aux.tile([P, 2, NODES], BF16, tag="aux")
+            for j2 in range(2):
+                for i in range(NODE_TILES):
+                    nc.tensor.matmul(
+                        pair[:, j2, i * P : (i + 1) * P],
+                        lhsT=c_sb[k][:, i, (jt + j2) * P : (jt + j2 + 1) * P],
+                        rhs=ident_bf16[:],
+                        start=True,
+                        stop=True,
+                    )
+                c_flipped[ct + j2] = pair[:, j2, :]
+
+        def gate_sigmoid(ct):
+            jt = ct % FEAT_TILES
             z = work.tile([P, NODES], F32, tag="z")
             nc.vector.scalar_tensor_tensor(
-                out=z[:], in0=f_input[:, jt, :], scalar=2.0, in1=acc[:], op0=MULT, op1=ADD
+                out=z[:], in0=f_input[:, jt, :], scalar=2.0, in1=sums[ct][:], op0=MULT, op1=ADD
             )
             f = work.tile([P, NODES], F32, tag="f")
             nc.scalar.activation(out=f[:], in_=z[:], func=SIGMOID, bias=bias_cols[:, ct : ct + 1], scale=1.0)
@@ -223,10 +243,15 @@ def tile_treelstmcell_pa_kernel(
                 adder = nc.vector if ct == COL_TILES - 1 else nc.gpsimd
                 adder.tensor_tensor(out=total[:, jt, :], in0=total[:, jt, :], in1=term[:], op=ADD)
 
-        gate(0)
-        for ct in range(1, COL_TILES):
-            gate(ct)
-            weigh_and_add(ct - 1)
+        for ct in range(COL_TILES):
+            gate_matmuls(ct)
+            if ct == 0:
+                compute_f_input()
+            if ct % 2 == 0:
+                flip_c_of_two_tiles(ct)
+            gate_sigmoid(ct)
+            if ct > 0:
+                weigh_and_add(ct - 1)
         weigh_and_add(COL_TILES - 1)
 
         out_view = out.rearrange("(p i) j -> p i j", i=NODE_TILES)

@@ -43,7 +43,6 @@ def tile_treelstmcell_pa_kernel(
 ):
     nc = tc.nc
     with ExitStack() as ctx:
-        ctx.enter_context(tc.manual_schedule())
         keep = ctx.enter_context(tc.tile_pool(name="keep", bufs=1))
         stage = ctx.enter_context(tc.tile_pool(name="stage", bufs=4))
         work = ctx.enter_context(tc.tile_pool(name="work", bufs=3))
@@ -102,6 +101,11 @@ def tile_treelstmcell_pa_kernel(
         nc.sync.dma_start(out=x_sb[:], in_=x.rearrange("(p i) k -> p i k", i=NODE_TILES))
         for i in range(NODE_TILES):
             nc.sync.dma_start(out=h_sb[i][:], in_=h_dram[:, i, :, :])
+        nc.sync.dma_start(out=wf_words[:].bitcast(I32), in_=W_f_in_words[0].bitcast(I32))
+        for r in range(4):
+            nc.sync.dma_start(
+                out=wf_scales[r:P:32, :].bitcast(I32), in_=W_f_in_scales[0, r:16:4, :].bitcast(I32)
+            )
         for k in range(CHILDREN):
             cols = slice(k * FP4_BYTES * FEAT, (k + 1) * FP4_BYTES * FEAT)
             nc.sync.dma_start(out=wa_words[k][:].bitcast(I32), in_=wa_words_dram[:, :, cols].bitcast(I32))
@@ -110,12 +114,6 @@ def tile_treelstmcell_pa_kernel(
                     out=wa_scales[r:P:32, :, k * FEAT : (k + 1) * FEAT].bitcast(I32),
                     in_=wa_scales_dram[r:16:4, :, k * FEAT : (k + 1) * FEAT].bitcast(I32),
                 )
-            if k == 0:
-                nc.sync.dma_start(out=wf_words[:].bitcast(I32), in_=W_f_in_words[0].bitcast(I32))
-                for r in range(4):
-                    nc.sync.dma_start(
-                        out=wf_scales[r:P:32, :].bitcast(I32), in_=W_f_in_scales[0, r:16:4, :].bitcast(I32)
-                    )
             nc.sync.dma_start(out=c_sb[k][:], in_=c_dram[:, :, k, :])
 
         units = []
@@ -127,37 +125,26 @@ def tile_treelstmcell_pa_kernel(
             for g in range(CHILDREN):
                 units.append((h_sb[i][:, g, :], h_codes[:, g, nodes], h_scales[:, g, nodes]))
 
-        banks = [units[first : first + 2] for first in range(0, len(units), 2)]
-        grouped_of_bank = {}
-
-        def flip_two_units(bank):
+        def quantise_two_units(two_units, copy_engine_is_vector):
             flipped = psum_aux.tile([P, 2, 2, P], F32, tag="aux")
             grouped = stage.tile([P, 2, K_PASS], BF16, tag="grouped", align_bytes=64)
             for a in range(2):
-                words = banks[bank][a][0].bitcast(F32)
+                words = two_units[a][0].bitcast(F32)
                 for u in range(2):
                     nc.tensor.transpose(flipped[:, a, u, :], words[:, u : K_PASS // 2 : 2], ident_f32[:])
             dst = grouped[:].bitcast(F32).rearrange("p a (n u) -> p a n u", u=2)
             src = flipped[:].rearrange("p a u n -> p a n u")
-            if bank % 3 == 2:
+            if copy_engine_is_vector:
                 nc.vector.tensor_copy(out=dst, in_=src)
             else:
                 nc.scalar.copy(out=dst, in_=src)
-            grouped_of_bank[bank] = grouped
-
-        def quantise_two_units(bank):
             for a in range(2):
                 nc.vector.quantize_mx(
-                    out=banks[bank][a][1].bitcast(FP8X4),
-                    scales=banks[bank][a][2],
-                    in_=grouped_of_bank[bank][:, a, :],
+                    out=two_units[a][1].bitcast(FP8X4), scales=two_units[a][2], in_=grouped[:, a, :]
                 )
 
-        for bank in range(len(banks)):
-            flip_two_units(bank)
-            if bank > 0:
-                quantise_two_units(bank - 1)
-        quantise_two_units(len(banks) - 1)
+        for bank in range(len(units) // 2):
+            quantise_two_units(units[2 * bank : 2 * bank + 2], bank % 3 == 2)
 
         bias_ps = psum_aux.tile([P, P], BF16, tag="aux")
         nc.tensor.transpose(bias_ps[:], bias_rows[:], ident_bf16[:])
@@ -169,32 +156,30 @@ def tile_treelstmcell_pa_kernel(
             in_=mask_ps[:].rearrange("q (p i) -> q i p", i=NODE_TILES),
         )
 
-        def compute_f_input():
-            for jt in range(FEAT_TILES):
-                acc = psum_aux.tile([P, NODES], F32, tag="aux")
-                nc.tensor.matmul_mx(
-                    out=acc[:],
-                    lhsT=wf_words[:, jt * FP4_BYTES * P : (jt + 1) * FP4_BYTES * P].bitcast(FP4X4),
-                    lhsT_scale=wf_scales[:, jt * P : (jt + 1) * P],
-                    rhs=x_codes[:].bitcast(FP8X4),
-                    rhs_scale=x_scales[:],
-                    start=True,
-                    stop=True,
-                )
-                nc.vector.scalar_tensor_tensor(
-                    out=f_input[:, jt, :],
-                    in0=acc[:],
-                    scalar=bias_cols[:, COL_TILES + jt : COL_TILES + jt + 1],
-                    in1=mask_all[:],
-                    op0=ADD,
-                    op1=MULT,
-                )
+        for jt in range(FEAT_TILES):
+            acc = psum_aux.tile([P, NODES], F32, tag="aux")
+            nc.tensor.matmul_mx(
+                out=acc[:],
+                lhsT=wf_words[:, jt * FP4_BYTES * P : (jt + 1) * FP4_BYTES * P].bitcast(FP4X4),
+                lhsT_scale=wf_scales[:, jt * P : (jt + 1) * P],
+                rhs=x_codes[:].bitcast(FP8X4),
+                rhs_scale=x_scales[:],
+                start=True,
+                stop=True,
+            )
+            nc.vector.scalar_tensor_tensor(
+                out=f_input[:, jt, :],
+                in0=acc[:],
+                scalar=bias_cols[:, COL_TILES + jt : COL_TILES + jt + 1],
+                in1=mask_all[:],
+                op0=ADD,
+                op1=MULT,
+            )
 
-        sums = {}
         gates = {}
         c_flipped = {}
 
-        def gate_matmuls(ct):
+        def gate(ct):
             k, jt = divmod(ct, FEAT_TILES)
             acc = psum_acc.tile([P, NODES], F32, tag="acc")
             for g in range(CHILDREN):
@@ -207,27 +192,21 @@ def tile_treelstmcell_pa_kernel(
                     start=(g == 0),
                     stop=(g == CHILDREN - 1),
                 )
-            sums[ct] = acc
-
-        def flip_c_of_two_tiles(ct):
-            k, jt = divmod(ct, FEAT_TILES)
-            pair = psum_aux.tile([P, 2, NODES], BF16, tag="aux")
-            for j2 in range(2):
-                for i in range(NODE_TILES):
-                    nc.tensor.matmul(
-                        pair[:, j2, i * P : (i + 1) * P],
-                        lhsT=c_sb[k][:, i, (jt + j2) * P : (jt + j2 + 1) * P],
-                        rhs=ident_bf16[:],
-                        start=True,
-                        stop=True,
-                    )
-                c_flipped[ct + j2] = pair[:, j2, :]
-
-        def gate_sigmoid(ct):
-            jt = ct % FEAT_TILES
+            if ct % 2 == 0:
+                pair = psum_aux.tile([P, 2, NODES], BF16, tag="aux")
+                for j2 in range(2):
+                    for i in range(NODE_TILES):
+                        nc.tensor.matmul(
+                            pair[:, j2, i * P : (i + 1) * P],
+                            lhsT=c_sb[k][:, i, (jt + j2) * P : (jt + j2 + 1) * P],
+                            rhs=ident_bf16[:],
+                            start=True,
+                            stop=True,
+                        )
+                    c_flipped[ct + j2] = pair[:, j2, :]
             z = work.tile([P, NODES], F32, tag="z")
             nc.vector.scalar_tensor_tensor(
-                out=z[:], in0=f_input[:, jt, :], scalar=2.0, in1=sums[ct][:], op0=MULT, op1=ADD
+                out=z[:], in0=f_input[:, jt, :], scalar=2.0, in1=acc[:], op0=MULT, op1=ADD
             )
             f = work.tile([P, NODES], F32, tag="f")
             nc.scalar.activation(out=f[:], in_=z[:], func=SIGMOID, bias=bias_cols[:, ct : ct + 1], scale=1.0)
@@ -243,15 +222,10 @@ def tile_treelstmcell_pa_kernel(
                 adder = nc.vector if ct == COL_TILES - 1 else nc.gpsimd
                 adder.tensor_tensor(out=total[:, jt, :], in0=total[:, jt, :], in1=term[:], op=ADD)
 
-        for ct in range(COL_TILES):
-            gate_matmuls(ct)
-            if ct == 0:
-                compute_f_input()
-            if ct % 2 == 0:
-                flip_c_of_two_tiles(ct)
-            gate_sigmoid(ct)
-            if ct > 0:
-                weigh_and_add(ct - 1)
+        gate(0)
+        for ct in range(1, COL_TILES):
+            gate(ct)
+            weigh_and_add(ct - 1)
         weigh_and_add(COL_TILES - 1)
 
         out_view = out.rearrange("(p i) j -> p i j", i=NODE_TILES)

@@ -46,6 +46,7 @@ def tile_treelstmcell_pa_kernel(
         keep = ctx.enter_context(tc.tile_pool(name="keep", bufs=1))
         stage = ctx.enter_context(tc.tile_pool(name="stage", bufs=4))
         work = ctx.enter_context(tc.tile_pool(name="work", bufs=3))
+        outgoing = ctx.enter_context(tc.tile_pool(name="outgoing", bufs=5))
         psum_acc = ctx.enter_context(tc.psum_pool(name="psum_acc", bufs=4))
         psum_aux = ctx.enter_context(tc.psum_pool(name="psum_aux", bufs=4))
 
@@ -98,6 +99,17 @@ def tile_treelstmcell_pa_kernel(
         wa_words_dram = W_aggr_f_words.rearrange("g p b -> p g b")
         wa_scales_dram = W_aggr_f_scales.rearrange("g q n -> q g n")
 
+        def load_wa_words(k):
+            cols = slice(k * FP4_BYTES * FEAT, (k + 1) * FP4_BYTES * FEAT)
+            nc.sync.dma_start(out=wa_words[k][:].bitcast(I32), in_=wa_words_dram[:, :, cols].bitcast(I32))
+
+        def load_wa_scales(k):
+            for r in range(4):
+                nc.sync.dma_start(
+                    out=wa_scales[r:P:32, :, k * FEAT : (k + 1) * FEAT].bitcast(I32),
+                    in_=wa_scales_dram[r:16:4, :, k * FEAT : (k + 1) * FEAT].bitcast(I32),
+                )
+
         nc.sync.dma_start(out=x_sb[:], in_=x.rearrange("(p i) k -> p i k", i=NODE_TILES))
         for i in range(NODE_TILES):
             nc.sync.dma_start(out=h_sb[i][:], in_=h_dram[:, i, :, :])
@@ -107,23 +119,17 @@ def tile_treelstmcell_pa_kernel(
                 out=wf_scales[r:P:32, :].bitcast(I32), in_=W_f_in_scales[0, r:16:4, :].bitcast(I32)
             )
         for k in range(CHILDREN):
-            cols = slice(k * FP4_BYTES * FEAT, (k + 1) * FP4_BYTES * FEAT)
-            nc.sync.dma_start(out=wa_words[k][:].bitcast(I32), in_=wa_words_dram[:, :, cols].bitcast(I32))
-            for r in range(4):
-                nc.sync.dma_start(
-                    out=wa_scales[r:P:32, :, k * FEAT : (k + 1) * FEAT].bitcast(I32),
-                    in_=wa_scales_dram[r:16:4, :, k * FEAT : (k + 1) * FEAT].bitcast(I32),
-                )
+            load_wa_words(k)
+            load_wa_scales(k)
             nc.sync.dma_start(out=c_sb[k][:], in_=c_dram[:, :, k, :])
 
-        units = []
+        x_units = []
+        h_units = []
         for i in range(NODE_TILES):
             nodes = slice(i * P, (i + 1) * P)
-            units.append((x_sb[:, i, :], x_codes[:, nodes], x_scales[:, nodes]))
-        for i in range(NODE_TILES):
-            nodes = slice(i * P, (i + 1) * P)
+            x_units.append((x_sb[:, i, :], x_codes[:, nodes], x_scales[:, nodes]))
             for g in range(CHILDREN):
-                units.append((h_sb[i][:, g, :], h_codes[:, g, nodes], h_scales[:, g, nodes]))
+                h_units.append((h_sb[i][:, g, :], h_codes[:, g, nodes], h_scales[:, g, nodes]))
 
         def quantise_two_units(two_units, copy_engine_is_vector):
             flipped = psum_aux.tile([P, 2, 2, P], F32, tag="aux")
@@ -143,43 +149,43 @@ def tile_treelstmcell_pa_kernel(
                     out=two_units[a][1].bitcast(FP8X4), scales=two_units[a][2], in_=grouped[:, a, :]
                 )
 
-        for bank in range(len(units) // 2):
-            quantise_two_units(units[2 * bank : 2 * bank + 2], bank % 3 == 2)
-
-        bias_ps = psum_aux.tile([P, P], BF16, tag="aux")
-        nc.tensor.transpose(bias_ps[:], bias_rows[:], ident_bf16[:])
-        nc.vector.tensor_copy(out=bias_cols[:], in_=bias_ps[:])
-        mask_ps = psum_aux.tile([P, NODES], F32, tag="aux")
-        nc.tensor.matmul(mask_ps[:], lhsT=ones_bf16[:], rhs=mask_row[:], start=True, stop=True)
-        nc.scalar.copy(
-            out=mask_all[:].rearrange("q (i p) -> q i p", i=NODE_TILES),
-            in_=mask_ps[:].rearrange("q (p i) -> q i p", i=NODE_TILES),
-        )
-
-        for jt in range(FEAT_TILES):
-            acc = psum_aux.tile([P, NODES], F32, tag="aux")
-            nc.tensor.matmul_mx(
-                out=acc[:],
-                lhsT=wf_words[:, jt * FP4_BYTES * P : (jt + 1) * FP4_BYTES * P].bitcast(FP4X4),
-                lhsT_scale=wf_scales[:, jt * P : (jt + 1) * P],
-                rhs=x_codes[:].bitcast(FP8X4),
-                rhs_scale=x_scales[:],
-                start=True,
-                stop=True,
-            )
-            nc.vector.scalar_tensor_tensor(
-                out=f_input[:, jt, :],
-                in0=acc[:],
-                scalar=bias_cols[:, COL_TILES + jt : COL_TILES + jt + 1],
-                in1=mask_all[:],
-                op0=ADD,
-                op1=MULT,
+        def prepare_bias_and_mask():
+            bias_ps = psum_aux.tile([P, P], BF16, tag="aux")
+            nc.tensor.transpose(bias_ps[:], bias_rows[:], ident_bf16[:])
+            nc.vector.tensor_copy(out=bias_cols[:], in_=bias_ps[:])
+            mask_ps = psum_aux.tile([P, NODES], F32, tag="aux")
+            nc.tensor.matmul(mask_ps[:], lhsT=ones_bf16[:], rhs=mask_row[:], start=True, stop=True)
+            nc.scalar.copy(
+                out=mask_all[:].rearrange("q (i p) -> q i p", i=NODE_TILES),
+                in_=mask_ps[:].rearrange("q (p i) -> q i p", i=NODE_TILES),
             )
 
+        def make_f_input():
+            for jt in range(FEAT_TILES):
+                acc = psum_aux.tile([P, NODES], F32, tag="aux")
+                nc.tensor.matmul_mx(
+                    out=acc[:],
+                    lhsT=wf_words[:, jt * FP4_BYTES * P : (jt + 1) * FP4_BYTES * P].bitcast(FP4X4),
+                    lhsT_scale=wf_scales[:, jt * P : (jt + 1) * P],
+                    rhs=x_codes[:].bitcast(FP8X4),
+                    rhs_scale=x_scales[:],
+                    start=True,
+                    stop=True,
+                )
+                nc.vector.scalar_tensor_tensor(
+                    out=f_input[:, jt, :],
+                    in0=acc[:],
+                    scalar=bias_cols[:, COL_TILES + jt : COL_TILES + jt + 1],
+                    in1=mask_all[:],
+                    op0=ADD,
+                    op1=MULT,
+                )
+
+        sums = {}
         gates = {}
         c_flipped = {}
 
-        def gate(ct):
+        def gate_passes(ct):
             k, jt = divmod(ct, FEAT_TILES)
             acc = psum_acc.tile([P, NODES], F32, tag="acc")
             for g in range(CHILDREN):
@@ -192,21 +198,27 @@ def tile_treelstmcell_pa_kernel(
                     start=(g == 0),
                     stop=(g == CHILDREN - 1),
                 )
-            if ct % 2 == 0:
-                pair = psum_aux.tile([P, 2, NODES], BF16, tag="aux")
-                for j2 in range(2):
-                    for i in range(NODE_TILES):
-                        nc.tensor.matmul(
-                            pair[:, j2, i * P : (i + 1) * P],
-                            lhsT=c_sb[k][:, i, (jt + j2) * P : (jt + j2 + 1) * P],
-                            rhs=ident_bf16[:],
-                            start=True,
-                            stop=True,
-                        )
-                    c_flipped[ct + j2] = pair[:, j2, :]
+            sums[ct] = acc
+
+        def flip_c(ct):
+            k, jt = divmod(ct, FEAT_TILES)
+            pair = psum_aux.tile([P, 2, NODES], BF16, tag="aux")
+            for j2 in range(2):
+                for i in range(NODE_TILES):
+                    nc.tensor.matmul(
+                        pair[:, j2, i * P : (i + 1) * P],
+                        lhsT=c_sb[k][:, i, (jt + j2) * P : (jt + j2 + 1) * P],
+                        rhs=ident_bf16[:],
+                        start=True,
+                        stop=True,
+                    )
+                c_flipped[ct + j2] = pair[:, j2, :]
+
+        def squash(ct):
+            jt = ct % FEAT_TILES
             z = work.tile([P, NODES], F32, tag="z")
             nc.vector.scalar_tensor_tensor(
-                out=z[:], in0=f_input[:, jt, :], scalar=2.0, in1=acc[:], op0=MULT, op1=ADD
+                out=z[:], in0=f_input[:, jt, :], scalar=2.0, in1=sums[ct][:], op0=MULT, op1=ADD
             )
             f = work.tile([P, NODES], F32, tag="f")
             nc.scalar.activation(out=f[:], in_=z[:], func=SIGMOID, bias=bias_cols[:, ct : ct + 1], scale=1.0)
@@ -222,20 +234,54 @@ def tile_treelstmcell_pa_kernel(
                 adder = nc.vector if ct == COL_TILES - 1 else nc.gpsimd
                 adder.tensor_tensor(out=total[:, jt, :], in0=total[:, jt, :], in1=term[:], op=ADD)
 
-        gate(0)
-        for ct in range(1, COL_TILES):
-            gate(ct)
-            weigh_and_add(ct - 1)
-        weigh_and_add(COL_TILES - 1)
-
+        units = x_units + h_units
+        for bank in range(len(units) // 2):
+            quantise_two_units(units[2 * bank : 2 * bank + 2], bank % 3 == 2)
+        prepare_bias_and_mask()
+        make_f_input()
         out_view = out.rearrange("(p i) j -> p i j", i=NODE_TILES)
-        for jt in range(FEAT_TILES):
-            back = psum_aux.tile([P, NODE_TILES, P], F32, tag="aux")
-            for i in range(NODE_TILES):
-                nc.tensor.transpose(back[:, i, :], total[:, jt, i * P : (i + 1) * P], ident_f32[:])
-            result = work.tile([P, NODE_TILES, P], F32, tag="result")
-            if jt % 2 == 0:
-                nc.scalar.copy(out=result[:], in_=back[:])
-            else:
+
+        def turn_back_and_store(jt, first_tile, n_tiles, copy_engine_is_vector):
+            back = psum_aux.tile([P, n_tiles, P], F32, tag="aux")
+            for i in range(n_tiles):
+                nodes = slice((first_tile + i) * P, (first_tile + i + 1) * P)
+                nc.tensor.transpose(back[:, i, :], total[:, jt, nodes], ident_f32[:])
+            result = outgoing.tile([P, n_tiles, P], F32, tag="result")
+            if copy_engine_is_vector:
                 nc.vector.tensor_copy(out=result[:], in_=back[:])
-            nc.sync.dma_start(out=out_view[:, :, jt * P : (jt + 1) * P], in_=result[:])
+            else:
+                nc.scalar.copy(out=result[:], in_=back[:])
+            nc.sync.dma_start(
+                out=out_view[:, first_tile : first_tile + n_tiles, jt * P : (jt + 1) * P], in_=result[:]
+            )
+
+        last = COL_TILES - 1
+        for ct in range(last):
+            gate_passes(ct)
+            if ct % 2 == 0:
+                flip_c(ct)
+            squash(ct)
+            if ct > 0:
+                weigh_and_add(ct - 1)
+        gate_passes(last)
+        weigh_and_add(last - 1)
+        jt = last % FEAT_TILES
+        half = NODES // 2
+        z = work.tile([P, NODES], F32, tag="z")
+        f = work.tile([P, NODES], F32, tag="f")
+        term = work.tile([P, NODES], F32, tag="term")
+        for b in range(2):
+            cols = slice(b * half, (b + 1) * half)
+            nc.vector.scalar_tensor_tensor(
+                out=z[:, cols], in0=f_input[:, jt, cols], scalar=2.0, in1=sums[last][:, cols], op0=MULT, op1=ADD
+            )
+            nc.scalar.activation(
+                out=f[:, cols], in_=z[:, cols], func=SIGMOID, bias=bias_cols[:, last : last + 1], scale=1.0
+            )
+        for jt_done in range(FEAT_TILES - 1):
+            turn_back_and_store(jt_done, 0, NODE_TILES, False)
+        for b in range(2):
+            cols = slice(b * half, (b + 1) * half)
+            nc.vector.tensor_tensor(out=term[:, cols], in0=f[:, cols], in1=c_flipped[last][:, cols], op=MULT)
+            nc.vector.tensor_tensor(out=total[:, jt, cols], in0=total[:, jt, cols], in1=term[:, cols], op=ADD)
+            turn_back_and_store(jt, b * NODE_TILES // 2, NODE_TILES // 2, True)

from contextlib import ExitStack

import concourse.mybir as mybir
from concourse.masks import make_identity

F32 = mybir.dt.float32
BF16 = mybir.dt.bfloat16
I32 = mybir.dt.int32
U32 = mybir.dt.uint32
U8 = mybir.dt.uint8
FP8X4 = mybir.dt.float8_e4m3fn_x4
FP4X4 = mybir.dt.float4_e2m1fn_x4
ADD = mybir.AluOpType.add
MULT = mybir.AluOpType.mult
SIGMOID = mybir.ActivationFunctionType.Sigmoid

P = 128
NODES = 512
CHILDREN = 5
FEAT = 512
K_PASS = 512
NODE_TILES = NODES // P
FEAT_TILES = FEAT // P
COL_TILES = CHILDREN * FEAT_TILES
FP4_BYTES = 2

FLOPS = 2 * NODES * (CHILDREN * FEAT) * (CHILDREN * FEAT) + 2 * NODES * FEAT * FEAT


def tile_treelstmcell_pa_kernel(
    tc,
    x,
    x_mask,
    neighbour_h,
    neighbour_c,
    W_f_in_words,
    W_f_in_scales,
    b_f_in,
    W_aggr_f_words,
    W_aggr_f_scales,
    b_aggr_f,
    out,
):
    nc = tc.nc
    with ExitStack() as ctx:
        keep = ctx.enter_context(tc.tile_pool(name="keep", bufs=1))
        stage = ctx.enter_context(tc.tile_pool(name="stage", bufs=4))
        work = ctx.enter_context(tc.tile_pool(name="work", bufs=3))
        outgoing = ctx.enter_context(tc.tile_pool(name="outgoing", bufs=5))
        psum_acc = ctx.enter_context(tc.psum_pool(name="psum_acc", bufs=4))
        psum_aux = ctx.enter_context(tc.psum_pool(name="psum_aux", bufs=4))

        ident_f32 = keep.tile([P, P], F32)
        ident_bf16 = keep.tile([P, P], BF16)
        ones_bf16 = keep.tile([P, P], BF16)
        bias_rows = keep.tile([P, P], BF16)
        bias_cols = keep.tile([P, P], F32)
        mask_row = keep.tile([P, NODES], BF16)
        mask_all = keep.tile([P, NODES], F32)
        warm = keep.tile([P, 1], F32)

        x_sb = keep.tile([P, NODE_TILES, FEAT], BF16)
        h_sb = [keep.tile([P, CHILDREN, FEAT], BF16, name="h_sb%d" % i) for i in range(NODE_TILES)]
        c_sb = [keep.tile([P, NODE_TILES, FEAT], BF16, name="c_sb%d" % k) for k in range(CHILDREN)]
        wf_words = keep.tile([P, FP4_BYTES * FEAT], U8, align_bytes=64)
        wf_scales = keep.tile([P, FEAT], U8, align_bytes=64)
        wa_words = [
            keep.tile([P, CHILDREN, FP4_BYTES * FEAT], U8, name="wa_words%d" % k, align_bytes=64)
            for k in range(CHILDREN)
        ]
        wa_scales = keep.tile([P, CHILDREN, CHILDREN * FEAT], U8, align_bytes=64)

        x_codes = keep.tile([P, NODES], U32, align_bytes=64)
        x_scales = keep.tile([P, NODES], U8, align_bytes=64)
        h_codes = keep.tile([P, CHILDREN, NODES], U32, align_bytes=64)
        h_scales = keep.tile([P, CHILDREN, NODES], U8, align_bytes=64)

        f_input = keep.tile([P, FEAT_TILES, NODES], F32)
        total = keep.tile([P, FEAT_TILES, NODES], F32)

        nc.vector.memset(warm[:], 0.0)
        nc.vector.memset(bias_rows[:], 0.0)
        nc.vector.memset(mask_row[:], 0.0)
        nc.vector.memset(wf_scales[:].bitcast(I32), 0)
        nc.vector.memset(wa_scales[:].rearrange("p g n -> p (g n)").bitcast(I32), 0)
        nc.vector.memset(ones_bf16[:], 1.0)
        make_identity(nc, ident_f32[:])
        make_identity(nc, ident_bf16[:])
        nc.scalar.activation(out=warm[:], in_=warm[:], func=SIGMOID)

        nc.gpsimd.dma_start(out=bias_rows[0:COL_TILES, :], in_=b_aggr_f.rearrange("(r c) -> r c", c=P))
        nc.gpsimd.dma_start(
            out=bias_rows[COL_TILES : COL_TILES + FEAT_TILES, :], in_=b_f_in.rearrange("(r c) -> r c", c=P)
        )
        nc.gpsimd.dma_start(out=mask_row[0:1, :], in_=x_mask.rearrange("(o n) -> o n", o=1))

        h_dram = neighbour_h.rearrange("(p i) g k -> p i g k", i=NODE_TILES)
        c_dram = neighbour_c.rearrange("(p i) k j -> p i k j", i=NODE_TILES)
        wa_words_dram = W_aggr_f_words.rearrange("g p b -> p g b")
        wa_scales_dram = W_aggr_f_scales.rearrange("g q n -> q g n")

        def load_wa_words(k):
            cols = slice(k * FP4_BYTES * FEAT, (k + 1) * FP4_BYTES * FEAT)
            nc.sync.dma_start(out=wa_words[k][:].bitcast(I32), in_=wa_words_dram[:, :, cols].bitcast(I32))

        def load_wa_scales(k):
            for r in range(4):
                nc.sync.dma_start(
                    out=wa_scales[r:P:32, :, k * FEAT : (k + 1) * FEAT].bitcast(I32),
                    in_=wa_scales_dram[r:16:4, :, k * FEAT : (k + 1) * FEAT].bitcast(I32),
                )

        nc.sync.dma_start(out=x_sb[:], in_=x.rearrange("(p i) k -> p i k", i=NODE_TILES))
        for i in range(NODE_TILES):
            nc.sync.dma_start(out=h_sb[i][:], in_=h_dram[:, i, :, :])
        nc.sync.dma_start(out=wf_words[:].bitcast(I32), in_=W_f_in_words[0].bitcast(I32))
        for r in range(4):
            nc.sync.dma_start(
                out=wf_scales[r:P:32, :].bitcast(I32), in_=W_f_in_scales[0, r:16:4, :].bitcast(I32)
            )
        for k in range(CHILDREN):
            load_wa_words(k)
            load_wa_scales(k)
            nc.sync.dma_start(out=c_sb[k][:], in_=c_dram[:, :, k, :])

        x_units = []
        h_units = []
        for i in range(NODE_TILES):
            nodes = slice(i * P, (i + 1) * P)
            x_units.append((x_sb[:, i, :], x_codes[:, nodes], x_scales[:, nodes]))
            for g in range(CHILDREN):
                h_units.append((h_sb[i][:, g, :], h_codes[:, g, nodes], h_scales[:, g, nodes]))

        def quantise_two_units(two_units, copy_engine_is_vector):
            flipped = psum_aux.tile([P, 2, 2, P], F32, tag="aux")
            grouped = stage.tile([P, 2, K_PASS], BF16, tag="grouped", align_bytes=64)
            for a in range(2):
                words = two_units[a][0].bitcast(F32)
                for u in range(2):
                    nc.tensor.transpose(flipped[:, a, u, :], words[:, u : K_PASS // 2 : 2], ident_f32[:])
            dst = grouped[:].bitcast(F32).rearrange("p a (n u) -> p a n u", u=2)
            src = flipped[:].rearrange("p a u n -> p a n u")
            if copy_engine_is_vector:
                nc.vector.tensor_copy(out=dst, in_=src)
            else:
                nc.scalar.copy(out=dst, in_=src)
            for a in range(2):
                nc.vector.quantize_mx(
                    out=two_units[a][1].bitcast(FP8X4), scales=two_units[a][2], in_=grouped[:, a, :]
                )

        def prepare_bias_and_mask():
            bias_ps = psum_aux.tile([P, P], BF16, tag="aux")
            nc.tensor.transpose(bias_ps[:], bias_rows[:], ident_bf16[:])
            nc.vector.tensor_copy(out=bias_cols[:], in_=bias_ps[:])
            mask_ps = psum_aux.tile([P, NODES], F32, tag="aux")
            nc.tensor.matmul(mask_ps[:], lhsT=ones_bf16[:], rhs=mask_row[:], start=True, stop=True)
            nc.scalar.copy(
                out=mask_all[:].rearrange("q (i p) -> q i p", i=NODE_TILES),
                in_=mask_ps[:].rearrange("q (p i) -> q i p", i=NODE_TILES),
            )

        def make_f_input():
            for jt in range(FEAT_TILES):
                acc = psum_aux.tile([P, NODES], F32, tag="aux")
                nc.tensor.matmul_mx(
                    out=acc[:],
                    lhsT=wf_words[:, jt * FP4_BYTES * P : (jt + 1) * FP4_BYTES * P].bitcast(FP4X4),
                    lhsT_scale=wf_scales[:, jt * P : (jt + 1) * P],
                    rhs=x_codes[:].bitcast(FP8X4),
                    rhs_scale=x_scales[:],
                    start=True,
                    stop=True,
                )
                nc.vector.scalar_tensor_tensor(
                    out=f_input[:, jt, :],
                    in0=acc[:],
                    scalar=bias_cols[:, COL_TILES + jt : COL_TILES + jt + 1],
                    in1=mask_all[:],
                    op0=ADD,
                    op1=MULT,
                )

        sums = {}
        gates = {}
        c_flipped = {}

        def gate_passes(ct):
            k, jt = divmod(ct, FEAT_TILES)
            acc = psum_acc.tile([P, NODES], F32, tag="acc")
            for g in range(CHILDREN):
                nc.tensor.matmul_mx(
                    out=acc[:],
                    lhsT=wa_words[k][:, g, jt * FP4_BYTES * P : (jt + 1) * FP4_BYTES * P].bitcast(FP4X4),
                    lhsT_scale=wa_scales[:, g, ct * P : (ct + 1) * P],
                    rhs=h_codes[:, g, :].bitcast(FP8X4),
                    rhs_scale=h_scales[:, g, :],
                    start=(g == 0),
                    stop=(g == CHILDREN - 1),
                )
            sums[ct] = acc

        def flip_c(ct):
            k, jt = divmod(ct, FEAT_TILES)
            pair = psum_aux.tile([P, 2, NODES], BF16, tag="aux")
            for j2 in range(2):
                for i in range(NODE_TILES):
                    nc.tensor.matmul(
                        pair[:, j2, i * P : (i + 1) * P],
                        lhsT=c_sb[k][:, i, (jt + j2) * P : (jt + j2 + 1) * P],
                        rhs=ident_bf16[:],
                        start=True,
                        stop=True,
                    )
                c_flipped[ct + j2] = pair[:, j2, :]

        def squash(ct):
            jt = ct % FEAT_TILES
            z = work.tile([P, NODES], F32, tag="z")
            nc.vector.scalar_tensor_tensor(
                out=z[:], in0=f_input[:, jt, :], scalar=2.0, in1=sums[ct][:], op0=MULT, op1=ADD
            )
            f = work.tile([P, NODES], F32, tag="f")
            nc.scalar.activation(out=f[:], in_=z[:], func=SIGMOID, bias=bias_cols[:, ct : ct + 1], scale=1.0)
            gates[ct] = f

        def weigh_and_add(ct):
            k, jt = divmod(ct, FEAT_TILES)
            if k == 0:
                nc.vector.tensor_tensor(out=total[:, jt, :], in0=gates[ct][:], in1=c_flipped[ct], op=MULT)
            else:
                term = work.tile([P, NODES], F32, tag="term")
                nc.vector.tensor_tensor(out=term[:], in0=gates[ct][:], in1=c_flipped[ct], op=MULT)
                adder = nc.vector if ct == COL_TILES - 1 else nc.gpsimd
                adder.tensor_tensor(out=total[:, jt, :], in0=total[:, jt, :], in1=term[:], op=ADD)

        units = x_units + h_units
        for bank in range(len(units) // 2):
            quantise_two_units(units[2 * bank : 2 * bank + 2], bank % 3 == 2)
        prepare_bias_and_mask()
        make_f_input()
        out_view = out.rearrange("(p i) j -> p i j", i=NODE_TILES)

        def turn_back_and_store(jt, first_tile, n_tiles, copy_engine_is_vector):
            back = psum_aux.tile([P, n_tiles, P], F32, tag="aux")
            for i in range(n_tiles):
                nodes = slice((first_tile + i) * P, (first_tile + i + 1) * P)
                nc.tensor.transpose(back[:, i, :], total[:, jt, nodes], ident_f32[:])
            result = outgoing.tile([P, n_tiles, P], F32, tag="result")
            if copy_engine_is_vector:
                nc.vector.tensor_copy(out=result[:], in_=back[:])
            else:
                nc.scalar.copy(out=result[:], in_=back[:])
            nc.sync.dma_start(
                out=out_view[:, first_tile : first_tile + n_tiles, jt * P : (jt + 1) * P], in_=result[:]
            )

        last = COL_TILES - 1
        for ct in range(last):
            gate_passes(ct)
            if ct % 2 == 0:
                flip_c(ct)
            squash(ct)
            if ct > 0:
                weigh_and_add(ct - 1)
        gate_passes(last)
        weigh_and_add(last - 1)
        jt = last % FEAT_TILES
        half = NODES // 2
        z = work.tile([P, NODES], F32, tag="z")
        f = work.tile([P, NODES], F32, tag="f")
        term = work.tile([P, NODES], F32, tag="term")
        for b in range(2):
            cols = slice(b * half, (b + 1) * half)
            nc.vector.scalar_tensor_tensor(
                out=z[:, cols], in0=f_input[:, jt, cols], scalar=2.0, in1=sums[last][:, cols], op0=MULT, op1=ADD
            )
            nc.scalar.activation(
                out=f[:, cols], in_=z[:, cols], func=SIGMOID, bias=bias_cols[:, last : last + 1], scale=1.0
            )
        for jt_done in range(FEAT_TILES - 1):
            turn_back_and_store(jt_done, 0, NODE_TILES, False)
        for b in range(2):
            cols = slice(b * half, (b + 1) * half)
            nc.vector.tensor_tensor(out=term[:, cols], in0=f[:, cols], in1=c_flipped[last][:, cols], op=MULT)
            nc.vector.tensor_tensor(out=total[:, jt, cols], in0=total[:, jt, cols], in1=term[:, cols], op=ADD)
            turn_back_and_store(jt, b * NODE_TILES // 2, NODE_TILES // 2, True)
